import numpy as np
import ml_dtypes


def mxq(x, axis, fmt="e4m3"):
    dtype, down = {"e4m3": (ml_dtypes.float8_e4m3fn, 7), "e5m2": (ml_dtypes.float8_e5m2, 14)}[fmt]
    v = np.moveaxis(np.asarray(x, np.float32).astype(ml_dtypes.bfloat16).astype(np.float64), axis, -1)
    blocks = v.reshape(v.shape[:-1] + (-1, 32))
    amax = np.abs(blocks).max(-1, keepdims=True)
    byte = np.maximum(np.where(amax > 0, np.frexp(amax)[1] - 1 + 127, 0) - down, 1)
    scale = np.exp2(byte - 127.0)
    codes = (blocks / scale).astype(np.float32).astype(dtype).astype(np.float64)
    return np.moveaxis((codes * scale).reshape(v.shape), -1, axis)


WIDE = False


def mx_kscale(k):
    if not WIDE:
        return np.ones(k)
    levels = np.array([10, -10, 5, -5, 0])
    if k % 512:
        return np.exp2(np.random.permutation(np.resize(levels, k // 32))).repeat(32)
    a = np.empty((k // 512, 16))
    for p in range(k // 512):
        a[p, :8] = np.random.permutation(np.resize(levels, 8))
        for g in range(8):
            far = levels[np.abs(levels - a[p, g]) >= 10]
            a[p, g + 8] = far[np.random.randint(len(far))]
    return np.exp2(a.ravel()).repeat(32)


BF16 = ml_dtypes.bfloat16


def bf(x):
    return np.asarray(x, np.float32).astype(BF16)


def f64(x):
    return np.asarray(x).astype(np.float64)


B, K, D, H1, H2, C = 256, 4, 2048, 1024, 512, 64
N = B * K


def setup_inputs():
    s = mx_kscale(D)
    return {"nf1": bf(np.random.standard_normal((N, D)) * s),
            "nf2": bf(np.random.standard_normal((N * K, D)) * s),
            "w1_0": bf(np.random.standard_normal((D, H1)) / np.sqrt(D) / s[:, None]),
            "w2_0": bf(np.random.standard_normal((D, H1)) / np.sqrt(D) / s[:, None])}


def sage_gcn(cur, neigh, w1, w2):
    b, d = cur.shape
    agg = neigh.reshape(b, -1, d).mean(axis=1)
    return np.maximum((mxq(cur, 1, "e4m3") @ mxq(w2, 0, "e4m3")) + (mxq(agg, 1, "e4m3") @ mxq(w1, 0, "e4m3")), 0.0)


def reference(nf1, nf2, w1_0, w2_0):
    return sage_gcn(f64(nf1), f64(nf2), f64(w1_0), f64(w2_0))

@@ -1,0 +1,235 @@
+from contextlib import ExitStack
+
+import concourse.mybir as mybir
+from concourse.masks import make_identity
+
+F32 = mybir.dt.float32
+BF16 = mybir.dt.bfloat16
+U32 = mybir.dt.uint32
+U8 = mybir.dt.uint8
+FP8X4 = mybir.dt.float8_e4m3fn_x4
+
+P = 128
+PACK = 4
+K_PASS = P * PACK
+PSUM_BANKS = 8
+N_TILE = 512
+
+NODES = 1024
+NEIGHBOURS = 4
+D = 2048
+H = 1024
+
+TILES = NODES // P
+PASSES = D // K_PASS
+OWN, AGG = 0, 1
+CHUNKS = 2 * PASSES
+HALVES = H // N_TILE
+NODES_PER_ROWS = P // NEIGHBOURS
+WORDS_PER_PASS = K_PASS // 2
+PASSES_PER_BANK = 2
+
+FIRST = PSUM_BANKS // HALVES
+ROW_BUFFERS = 4
+W_ROW_BUFFERS = 4
+
+FLOPS = 2 * 2 * NODES * D * H
+
+
+def tile_graphsage_pa_kernel(tc, nf1, nf2, w1_0, w2_0, out):
+    nc = tc.nc
+
+    own_view = nf1.rearrange("(m p) d -> m p d", p=P)
+    neigh_view = nf2.rearrange("(m q p) d -> m p q d", q=NEIGHBOURS, p=P)
+    out_view = out.rearrange("(m p) h -> m p h", p=P)
+    own_w_view = w2_0.rearrange("(g p t) n -> g p t n", t=PACK, p=P)
+    agg_w_view = w1_0.rearrange("(g p t) n -> g p t n", t=PACK, p=P)
+
+    with ExitStack() as ctx:
+        const = ctx.enter_context(tc.tile_pool(name="const", bufs=1))
+        keep = ctx.enter_context(tc.tile_pool(name="keep", bufs=1))
+        rows_pool = ctx.enter_context(tc.tile_pool(name="rows", bufs=ROW_BUFFERS))
+        w_rows_pool = ctx.enter_context(tc.tile_pool(name="w_rows", bufs=W_ROW_BUFFERS))
+        w_grouped_pool = ctx.enter_context(tc.tile_pool(name="w_grouped", bufs=3))
+        own_grouped_pool = ctx.enter_context(tc.tile_pool(name="own_grouped", bufs=2))
+        agg_grouped_pool = ctx.enter_context(tc.tile_pool(name="agg_grouped", bufs=4))
+        agg_mx_pool = ctx.enter_context(tc.tile_pool(name="agg_mx", bufs=2))
+        banks = ctx.enter_context(tc.psum_pool(name="banks", bufs=PSUM_BANKS))
+        ctx.enter_context(tc.manual_schedule())
+
+        ident = const.tile([P, P], F32)
+        make_identity(nc, ident[:])
+        mean_f32 = const.tile([P, NODES_PER_ROWS], F32)
+        nc.vector.tensor_reduce(
+            out=mean_f32[:],
+            in_=ident[:].rearrange("p (i j) -> p i j", j=NEIGHBOURS),
+            axis=mybir.AxisListType.X,
+            op=mybir.AluOpType.add,
+        )
+        mean_cols = const.tile([P, NODES_PER_ROWS], BF16)
+        nc.vector.tensor_scalar_mul(out=mean_cols[:], in0=mean_f32[:], scalar1=1.0 / NEIGHBOURS)
+
+        w_codes = keep.tile([P, CHUNKS, H], U32, align_bytes=64)
+        w_scales = keep.tile([P, CHUNKS, H], U8, align_bytes=64)
+        own_codes = keep.tile([P, TILES, PASSES, P], U32, align_bytes=64)
+        own_scales = keep.tile([P, TILES, PASSES, P], U8, align_bytes=64)
+        result = keep.tile([P, TILES, H], F32)
+
+        own_rows, neigh_rows, w_rows, w_grouped = {}, {}, {}, {}
+        x_codes, x_scales, acc = {}, {}, {}
+
+        def load_own_rows(first_tile):
+            row_buffer = rows_pool.tile([P, NEIGHBOURS, D], BF16)
+            for j in range(NEIGHBOURS):
+                own_rows[first_tile + j] = row_buffer[:, j, :]
+                nc.sync.dma_start(out=row_buffer[:, j, :], in_=own_view[first_tile + j])
+
+        def load_neigh_rows(m):
+            row_buffer = rows_pool.tile([P, NEIGHBOURS, D], BF16)
+            neigh_rows[m] = row_buffer
+            nc.sync.dma_start(out=row_buffer[:], in_=neigh_view[m])
+
+        def load_weight_chunk(c):
+            w_rows[c] = w_rows_pool.tile([P, PACK, H], BF16, name="w_rows")
+            view = own_w_view[c] if c < PASSES else agg_w_view[c - PASSES]
+            nc.sync.dma_start(out=w_rows[c][:], in_=view)
+
+        def regroup_weight_chunk(c):
+            w_grouped[c] = w_grouped_pool.tile([P, H, PACK], BF16, name="w_grouped", align_bytes=64)
+            grouped = w_grouped[c][:].rearrange("p (a i) t -> p a t i", i=4)
+            rows = w_rows[c][:].rearrange("p t (a i) -> p a t i", i=4)
+            middle = H // 4 // 2
+            nc.vector.tensor_copy(out=grouped[:, :middle], in_=rows[:, :middle])
+            nc.scalar.copy(out=grouped[:, middle:], in_=rows[:, middle:])
+
+        def quantise_weight_chunk(c):
+            if c + 1 < CHUNKS:
+                regroup_weight_chunk(c + 1)
+            nc.vector.quantize_mx(
+                out=w_codes[:, c, :].bitcast(FP8X4),
+                scales=w_scales[:, c, :],
+                in_=w_grouped[c][:].rearrange("p n t -> p (n t)"),
+            )
+            if c + W_ROW_BUFFERS < CHUNKS:
+                load_weight_chunk(c + W_ROW_BUFFERS)
+
+        def prepare_own(m):
+            row_words = own_rows[m].bitcast(F32)
+            own_grouped = own_grouped_pool.tile([P, PASSES * P * PACK], BF16, align_bytes=64)
+            grouped_words = own_grouped[:].bitcast(F32).rearrange(
+                "p (g r u) -> p g r u", g=PASSES, u=2
+            )
+            for first_pass in range(0, PASSES, PASSES_PER_BANK):
+                own_bank = banks.tile([P, PASSES_PER_BANK, 2, P], F32, tag="bank")
+                for i in range(PASSES_PER_BANK):
+                    for u in range(2):
+                        first_word = (first_pass + i) * WORDS_PER_PASS
+                        nc.tensor.transpose(
+                            own_bank[:, i, u, :],
+                            row_words[:, first_word + u : first_word + WORDS_PER_PASS : 2],
+                            ident[:],
+                        )
+                nc.scalar.copy(
+                    out=grouped_words[:, first_pass : first_pass + PASSES_PER_BANK],
+                    in_=own_bank[:].rearrange("p g u r -> p g r u"),
+                )
+            x_codes[m, OWN] = own_codes[:, m]
+            x_scales[m, OWN] = own_scales[:, m]
+            nc.vector.quantize_mx(
+                out=x_codes[m, OWN].rearrange("p g r -> p (g r)").bitcast(FP8X4),
+                scales=x_scales[m, OWN].rearrange("p g r -> p (g r)"),
+                in_=own_grouped[:],
+            )
+
+        def prepare_agg(m, g):
+            if g == 0:
+                agg_codes = agg_mx_pool.tile([P, PASSES, P], U32, align_bytes=64)
+                agg_scales = agg_mx_pool.tile([P, PASSES, P], U8, align_bytes=64)
+                x_codes[m, AGG] = agg_codes[:]
+                x_scales[m, AGG] = agg_scales[:]
+            agg_bank = banks.tile([P, PACK, P], F32, tag="bank")
+            for q in range(NEIGHBOURS):
+                nodes = slice(q * NODES_PER_ROWS, (q + 1) * NODES_PER_ROWS)
+                for t in range(PACK):
+                    first_d = g * K_PASS
+                    nc.tensor.matmul(
+                        out=agg_bank[:, t, nodes],
+                        lhsT=neigh_rows[m][:, q, first_d + t : first_d + K_PASS : PACK],
+                        rhs=mean_cols[:],
+                        start=True,
+                        stop=True,
+                    )
+            agg_grouped = agg_grouped_pool.tile([P, P, PACK], BF16, align_bytes=64)
+            nc.scalar.copy(out=agg_grouped[:], in_=agg_bank[:].rearrange("p t r -> p r t"))
+            nc.vector.quantize_mx(
+                out=x_codes[m, AGG][:, g, :].bitcast(FP8X4),
+                scales=x_scales[m, AGG][:, g, :],
+                in_=agg_grouped[:].rearrange("p r t -> p (r t)"),
+            )
+
+        def multiply(m, product, g):
+            if g == 0:
+                acc[m, product] = [
+                    banks.tile([P, N_TILE], F32, name="acc", tag="bank") for half in range(HALVES)
+                ]
+            c = PASSES * product + g
+            for half in range(HALVES):
+                cols = slice(half * N_TILE, (half + 1) * N_TILE)
+                nc.tensor.matmul_mx(
+                    out=acc[m, product][half][:],
+                    lhsT=x_codes[m, product][:, g, :].bitcast(FP8X4),
+                    lhsT_scale=x_scales[m, product][:, g, :],
+                    rhs=w_codes[:, c, cols].bitcast(FP8X4),
+                    rhs_scale=w_scales[:, c, cols],
+                    start=(g == 0),
+                    stop=(g == PASSES - 1),
+                )
+
+        def set_aside(m):
+            nc.vector.tensor_copy(out=result[:, m, 0:N_TILE], in_=acc[m, OWN][0][:])
+            nc.scalar.copy(out=result[:, m, N_TILE:H], in_=acc[m, OWN][1][:])
+
+        def finish(m):
+            for half in range(HALVES):
+                cols = slice(half * N_TILE, (half + 1) * N_TILE)
+                nc.vector.tensor_add(
+                    out=result[:, m, cols], in0=acc[m, AGG][half][:], in1=result[:, m, cols]
+                )
+            nc.vector.tensor_scalar_max(out=result[:, m, :], in0=result[:, m, :], scalar1=0.0)
+
+        for first_tile in range(0, TILES, NEIGHBOURS):
+            load_own_rows(first_tile)
+        for m in range(TILES):
+            prepare_own(m)
+
+        for c in range(W_ROW_BUFFERS):
+            load_weight_chunk(c)
+        regroup_weight_chunk(0)
+        for g in range(PASSES):
+            quantise_weight_chunk(PASSES * OWN + g)
+            for m in range(FIRST):
+                multiply(m, OWN, g)
+        for m in range(FIRST):
+            set_aside(m)
+        for g in range(PASSES):
+            quantise_weight_chunk(PASSES * AGG + g)
+        for m in range(FIRST, TILES):
+            for g in range(PASSES):
+                multiply(m, OWN, g)
+            set_aside(m)
+
+        for m in range(ROW_BUFFERS):
+            load_neigh_rows(m)
+        for m in range(TILES):
+            for g in range(PASSES):
+                prepare_agg(m, g)
+            if m + ROW_BUFFERS < TILES:
+                load_neigh_rows(m + ROW_BUFFERS)
+            if m > 0:
+                finish(m - 1)
+            for g in range(PASSES):
+                multiply(m, AGG, g)
+        finish(TILES - 1)
+
+        for m in range(TILES):
+            nc.sync.dma_start(out=out_view[m], in_=result[:, m, :])

@@ -105,13 +105,16 @@ def tile_graphsage_pa_kernel(tc, nf1, nf2, w1_0, w2_0, out):
         def quantise_weight_chunk(c):
             if c + 1 < CHUNKS:
                 regroup_weight_chunk(c + 1)
+            quantise_grouped_chunk(c)
+            if c + W_ROW_BUFFERS < CHUNKS:
+                load_weight_chunk(c + W_ROW_BUFFERS)
+
+        def quantise_grouped_chunk(c):
             nc.vector.quantize_mx(
                 out=w_codes[:, c, :].bitcast(FP8X4),
                 scales=w_scales[:, c, :],
                 in_=w_grouped[c][:].rearrange("p n t -> p (n t)"),
             )
-            if c + W_ROW_BUFFERS < CHUNKS:
-                load_weight_chunk(c + W_ROW_BUFFERS)
 
         def prepare_own(m):
             row_words = own_rows[m].bitcast(F32)
@@ -197,16 +200,24 @@ def tile_graphsage_pa_kernel(tc, nf1, nf2, w1_0, w2_0, out):
                 )
             nc.vector.tensor_scalar_max(out=result[:, m, :], in0=result[:, m, :], scalar1=0.0)
 
-        for first_tile in range(0, TILES, NEIGHBOURS):
-            load_own_rows(first_tile)
-        for m in range(TILES):
+        load_own_rows(0)
+        load_weight_chunk(0)
+        load_own_rows(NEIGHBOURS)
+        for c in range(1, W_ROW_BUFFERS):
+            load_weight_chunk(c)
+        for m in range(NEIGHBOURS):
+            prepare_own(m)
+        regroup_weight_chunk(0)
+        prepare_own(NEIGHBOURS)
+        quantise_grouped_chunk(0)
+        for m in range(NEIGHBOURS + 1, TILES):
             prepare_own(m)
 
-        for c in range(W_ROW_BUFFERS):
-            load_weight_chunk(c)
-        regroup_weight_chunk(0)
+        regroup_weight_chunk(1)
+        load_weight_chunk(W_ROW_BUFFERS)
         for g in range(PASSES):
-            quantise_weight_chunk(PASSES * OWN + g)
+            if g > 0:
+                quantise_weight_chunk(PASSES * OWN + g)
             for m in range(FIRST):
                 multiply(m, OWN, g)
         for m in range(FIRST):
@@ -220,16 +231,16 @@ def tile_graphsage_pa_kernel(tc, nf1, nf2, w1_0, w2_0, out):
 
         for m in range(ROW_BUFFERS):
             load_neigh_rows(m)
-        for m in range(TILES):
-            for g in range(PASSES):
-                prepare_agg(m, g)
-            if m + ROW_BUFFERS < TILES:
-                load_neigh_rows(m + ROW_BUFFERS)
+        for m in range(TILES + 1):
+            if m < TILES:
+                for g in range(PASSES):
+                    prepare_agg(m, g)
+                if m + ROW_BUFFERS < TILES:
+                    load_neigh_rows(m + ROW_BUFFERS)
             if m > 0:
+                for g in range(PASSES):
+                    multiply(m - 1, AGG, g)
                 finish(m - 1)
-            for g in range(PASSES):
-                multiply(m, AGG, g)
-        finish(TILES - 1)
 
         for m in range(TILES):
             nc.sync.dma_start(out=out_view[m], in_=result[:, m, :])

@@ -51,7 +51,7 @@ def tile_graphsage_pa_kernel(tc, nf1, nf2, w1_0, w2_0, out):
         rows_pool = ctx.enter_context(tc.tile_pool(name="rows", bufs=ROW_BUFFERS))
         w_rows_pool = ctx.enter_context(tc.tile_pool(name="w_rows", bufs=W_ROW_BUFFERS))
         w_grouped_pool = ctx.enter_context(tc.tile_pool(name="w_grouped", bufs=3))
-        own_grouped_pool = ctx.enter_context(tc.tile_pool(name="own_grouped", bufs=2))
+        own_grouped_pool = ctx.enter_context(tc.tile_pool(name="own_grouped", bufs=3))
         agg_grouped_pool = ctx.enter_context(tc.tile_pool(name="agg_grouped", bufs=4))
         agg_mx_pool = ctx.enter_context(tc.tile_pool(name="agg_mx", bufs=2))
         banks = ctx.enter_context(tc.psum_pool(name="banks", bufs=PSUM_BANKS))
@@ -75,7 +75,7 @@ def tile_graphsage_pa_kernel(tc, nf1, nf2, w1_0, w2_0, out):
         own_scales = keep.tile([P, TILES, PASSES, P], U8, align_bytes=64)
         result = keep.tile([P, TILES, H], F32)
 
-        own_rows, neigh_rows, w_rows, w_grouped = {}, {}, {}, {}
+        own_rows, neigh_rows, w_rows, w_grouped, own_grouped = {}, {}, {}, {}, {}
         x_codes, x_scales, acc = {}, {}, {}
 
         def load_own_rows(first_tile):
@@ -103,7 +103,7 @@ def tile_graphsage_pa_kernel(tc, nf1, nf2, w1_0, w2_0, out):
             nc.scalar.copy(out=grouped[:, middle:], in_=rows[:, middle:])
 
         def quantise_weight_chunk(c):
-            if c + 1 < CHUNKS:
+            if PASSES <= c < CHUNKS - 1:
                 regroup_weight_chunk(c + 1)
             quantise_grouped_chunk(c)
             if c + W_ROW_BUFFERS < CHUNKS:
@@ -116,10 +116,12 @@ def tile_graphsage_pa_kernel(tc, nf1, nf2, w1_0, w2_0, out):
                 in_=w_grouped[c][:].rearrange("p n t -> p (n t)"),
             )
 
-        def prepare_own(m):
+        def transpose_own(m):
             row_words = own_rows[m].bitcast(F32)
-            own_grouped = own_grouped_pool.tile([P, PASSES * P * PACK], BF16, align_bytes=64)
-            grouped_words = own_grouped[:].bitcast(F32).rearrange(
+            own_grouped[m] = own_grouped_pool.tile(
+                [P, PASSES * P * PACK], BF16, name="own_grouped", align_bytes=64
+            )
+            grouped_words = own_grouped[m][:].bitcast(F32).rearrange(
                 "p (g r u) -> p g r u", g=PASSES, u=2
             )
             for first_pass in range(0, PASSES, PASSES_PER_BANK):
@@ -132,16 +134,20 @@ def tile_graphsage_pa_kernel(tc, nf1, nf2, w1_0, w2_0, out):
                             row_words[:, first_word + u : first_word + WORDS_PER_PASS : 2],
                             ident[:],
                         )
-                nc.scalar.copy(
+                on_vector = m < NEIGHBOURS and first_pass > 0
+                copy = nc.vector.tensor_copy if on_vector else nc.scalar.copy
+                copy(
                     out=grouped_words[:, first_pass : first_pass + PASSES_PER_BANK],
                     in_=own_bank[:].rearrange("p g u r -> p g r u"),
                 )
+
+        def quantise_own(m):
             x_codes[m, OWN] = own_codes[:, m]
             x_scales[m, OWN] = own_scales[:, m]
             nc.vector.quantize_mx(
                 out=x_codes[m, OWN].rearrange("p g r -> p (g r)").bitcast(FP8X4),
                 scales=x_scales[m, OWN].rearrange("p g r -> p (g r)"),
-                in_=own_grouped[:],
+                in_=own_grouped[m][:],
             )
 
         def prepare_agg(m, g):
@@ -205,21 +211,24 @@ def tile_graphsage_pa_kernel(tc, nf1, nf2, w1_0, w2_0, out):
         load_own_rows(NEIGHBOURS)
         for c in range(1, W_ROW_BUFFERS):
             load_weight_chunk(c)
-        for m in range(NEIGHBOURS):
-            prepare_own(m)
-        regroup_weight_chunk(0)
-        prepare_own(NEIGHBOURS)
-        quantise_grouped_chunk(0)
-        for m in range(NEIGHBOURS + 1, TILES):
-            prepare_own(m)
+        for m in range(TILES):
+            transpose_own(m)
+            if m > 0:
+                quantise_own(m - 1)
+            if m == NEIGHBOURS - 1:
+                regroup_weight_chunk(0)
+            if m == NEIGHBOURS + 1:
+                quantise_grouped_chunk(0)
+        quantise_own(TILES - 1)
 
-        regroup_weight_chunk(1)
         load_weight_chunk(W_ROW_BUFFERS)
         for g in range(PASSES):
             if g > 0:
-                quantise_weight_chunk(PASSES * OWN + g)
+                regroup_weight_chunk(g)
+                quantise_weight_chunk(g)
             for m in range(FIRST):
                 multiply(m, OWN, g)
+        regroup_weight_chunk(PASSES)
         for m in range(FIRST):
             set_aside(m)
         for g in range(PASSES):

@@ -29,9 +29,10 @@ NODES_PER_ROWS = P // NEIGHBOURS
 WORDS_PER_PASS = K_PASS // 2
 PASSES_PER_BANK = 2
 
-FIRST = PSUM_BANKS // HALVES
 ROW_BUFFERS = 4
 W_ROW_BUFFERS = 4
+FIRST = PSUM_BANKS // HALVES
+EARLY = {1: 0, 3: 1}
 
 FLOPS = 2 * 2 * NODES * D * H
 
@@ -50,7 +51,7 @@ def tile_graphsage_pa_kernel(tc, nf1, nf2, w1_0, w2_0, out):
         keep = ctx.enter_context(tc.tile_pool(name="keep", bufs=1))
         rows_pool = ctx.enter_context(tc.tile_pool(name="rows", bufs=ROW_BUFFERS))
         w_rows_pool = ctx.enter_context(tc.tile_pool(name="w_rows", bufs=W_ROW_BUFFERS))
-        w_grouped_pool = ctx.enter_context(tc.tile_pool(name="w_grouped", bufs=3))
+        w_grouped_pool = ctx.enter_context(tc.tile_pool(name="w_grouped", bufs=6))
         own_grouped_pool = ctx.enter_context(tc.tile_pool(name="own_grouped", bufs=3))
         agg_grouped_pool = ctx.enter_context(tc.tile_pool(name="agg_grouped", bufs=4))
         agg_mx_pool = ctx.enter_context(tc.tile_pool(name="agg_mx", bufs=2))
@@ -78,11 +79,12 @@ def tile_graphsage_pa_kernel(tc, nf1, nf2, w1_0, w2_0, out):
         own_rows, neigh_rows, w_rows, w_grouped, own_grouped = {}, {}, {}, {}, {}
         x_codes, x_scales, acc = {}, {}, {}
 
-        def load_own_rows(first_tile):
-            row_buffer = rows_pool.tile([P, NEIGHBOURS, D], BF16)
-            for j in range(NEIGHBOURS):
-                own_rows[first_tile + j] = row_buffer[:, j, :]
-                nc.sync.dma_start(out=row_buffer[:, j, :], in_=own_view[first_tile + j])
+        def load_own_rows(m):
+            if m % NEIGHBOURS == 0:
+                row_buffer = rows_pool.tile([P, NEIGHBOURS, D], BF16)
+                for j in range(NEIGHBOURS):
+                    own_rows[m + j] = row_buffer[:, j, :]
+            nc.sync.dma_start(out=own_rows[m], in_=own_view[m])
 
         def load_neigh_rows(m):
             row_buffer = rows_pool.tile([P, NEIGHBOURS, D], BF16)
@@ -90,30 +92,29 @@ def tile_graphsage_pa_kernel(tc, nf1, nf2, w1_0, w2_0, out):
             nc.sync.dma_start(out=row_buffer[:], in_=neigh_view[m])
 
         def load_weight_chunk(c):
-            w_rows[c] = w_rows_pool.tile([P, PACK, H], BF16, name="w_rows")
-            view = own_w_view[c] if c < PASSES else agg_w_view[c - PASSES]
-            nc.sync.dma_start(out=w_rows[c][:], in_=view)
+            rows = w_rows_pool.tile([P, PACK, H], BF16)
+            for half in range(HALVES):
+                w_rows[c, half] = rows[:, :, half * N_TILE : (half + 1) * N_TILE]
+            nc.sync.dma_start(
+                out=rows[:], in_=own_w_view[c] if c < PASSES else agg_w_view[c - PASSES]
+            )
 
-        def regroup_weight_chunk(c):
-            w_grouped[c] = w_grouped_pool.tile([P, H, PACK], BF16, name="w_grouped", align_bytes=64)
-            grouped = w_grouped[c][:].rearrange("p (a i) t -> p a t i", i=4)
-            rows = w_rows[c][:].rearrange("p t (a i) -> p a t i", i=4)
-            middle = H // 4 // 2
+        def regroup_weights(c, half):
+            w_grouped[c, half] = w_grouped_pool.tile(
+                [P, N_TILE, PACK], BF16, name="w_grouped", align_bytes=64
+            )
+            grouped = w_grouped[c, half][:].rearrange("p (a i) t -> p a t i", i=4)
+            rows = w_rows[c, half].rearrange("p t (a i) -> p a t i", i=4)
+            middle = N_TILE // 4 // 2
             nc.vector.tensor_copy(out=grouped[:, :middle], in_=rows[:, :middle])
             nc.scalar.copy(out=grouped[:, middle:], in_=rows[:, middle:])
 
-        def quantise_weight_chunk(c):
-            if PASSES <= c < CHUNKS - 1:
-                regroup_weight_chunk(c + 1)
-            quantise_grouped_chunk(c)
-            if c + W_ROW_BUFFERS < CHUNKS:
-                load_weight_chunk(c + W_ROW_BUFFERS)
-
-        def quantise_grouped_chunk(c):
+        def quantise_weights(c, half):
+            cols = slice(half * N_TILE, (half + 1) * N_TILE)
             nc.vector.quantize_mx(
-                out=w_codes[:, c, :].bitcast(FP8X4),
-                scales=w_scales[:, c, :],
-                in_=w_grouped[c][:].rearrange("p n t -> p (n t)"),
+                out=w_codes[:, c, cols].bitcast(FP8X4),
+                scales=w_scales[:, c, cols],
+                in_=w_grouped[c, half][:].rearrange("p n t -> p (n t)"),
             )
 
         def transpose_own(m):
@@ -134,7 +135,7 @@ def tile_graphsage_pa_kernel(tc, nf1, nf2, w1_0, w2_0, out):
                             row_words[:, first_word + u : first_word + WORDS_PER_PASS : 2],
                             ident[:],
                         )
-                on_vector = m < NEIGHBOURS and first_pass > 0
+                on_vector = m % 2 == 0 and first_pass > 0
                 copy = nc.vector.tensor_copy if on_vector else nc.scalar.copy
                 copy(
                     out=grouped_words[:, first_pass : first_pass + PASSES_PER_BANK],
@@ -176,80 +177,106 @@ def tile_graphsage_pa_kernel(tc, nf1, nf2, w1_0, w2_0, out):
                 in_=agg_grouped[:].rearrange("p r t -> p (r t)"),
             )
 
-        def multiply(m, product, g):
+        def multiply(m, product, g, half):
             if g == 0:
-                acc[m, product] = [
-                    banks.tile([P, N_TILE], F32, name="acc", tag="bank") for half in range(HALVES)
-                ]
+                acc[m, product, half] = banks.tile([P, N_TILE], F32, name="acc", tag="bank")
             c = PASSES * product + g
-            for half in range(HALVES):
-                cols = slice(half * N_TILE, (half + 1) * N_TILE)
-                nc.tensor.matmul_mx(
-                    out=acc[m, product][half][:],
-                    lhsT=x_codes[m, product][:, g, :].bitcast(FP8X4),
-                    lhsT_scale=x_scales[m, product][:, g, :],
-                    rhs=w_codes[:, c, cols].bitcast(FP8X4),
-                    rhs_scale=w_scales[:, c, cols],
-                    start=(g == 0),
-                    stop=(g == PASSES - 1),
-                )
+            cols = slice(half * N_TILE, (half + 1) * N_TILE)
+            nc.tensor.matmul_mx(
+                out=acc[m, product, half][:],
+                lhsT=x_codes[m, product][:, g, :].bitcast(FP8X4),
+                lhsT_scale=x_scales[m, product][:, g, :],
+                rhs=w_codes[:, c, cols].bitcast(FP8X4),
+                rhs_scale=w_scales[:, c, cols],
+                start=(g == 0),
+                stop=(g == PASSES - 1),
+            )
 
         def set_aside(m):
-            nc.vector.tensor_copy(out=result[:, m, 0:N_TILE], in_=acc[m, OWN][0][:])
-            nc.scalar.copy(out=result[:, m, N_TILE:H], in_=acc[m, OWN][1][:])
+            nc.vector.tensor_copy(out=result[:, m, 0:N_TILE], in_=acc[m, OWN, 0][:])
+            nc.scalar.copy(out=result[:, m, N_TILE:H], in_=acc[m, OWN, 1][:])
 
-        def finish(m):
-            for half in range(HALVES):
-                cols = slice(half * N_TILE, (half + 1) * N_TILE)
-                nc.vector.tensor_add(
-                    out=result[:, m, cols], in0=acc[m, AGG][half][:], in1=result[:, m, cols]
-                )
-            nc.vector.tensor_scalar_max(out=result[:, m, :], in0=result[:, m, :], scalar1=0.0)
+        def finish(m, half):
+            cols = slice(half * N_TILE, (half + 1) * N_TILE)
+            nc.vector.tensor_add(
+                out=result[:, m, cols], in0=acc[m, AGG, half][:], in1=result[:, m, cols]
+            )
 
-        load_own_rows(0)
-        load_weight_chunk(0)
-        load_own_rows(NEIGHBOURS)
-        for c in range(1, W_ROW_BUFFERS):
+        def rectify(m, cols):
+            nc.vector.tensor_scalar_max(
+                out=result[:, m, cols], in0=result[:, m, cols], scalar1=0.0
+            )
+
+        for m in range(TILES):
+            if m in EARLY:
+                load_weight_chunk(EARLY[m])
+            load_own_rows(m)
+        for c in range(len(EARLY), CHUNKS):
             load_weight_chunk(c)
+        for m in range(TILES):
+            load_neigh_rows(m)
+
         for m in range(TILES):
             transpose_own(m)
             if m > 0:
                 quantise_own(m - 1)
-            if m == NEIGHBOURS - 1:
-                regroup_weight_chunk(0)
-            if m == NEIGHBOURS + 1:
-                quantise_grouped_chunk(0)
+            if m + 1 in EARLY:
+                regroup_weights(EARLY[m + 1], 0)
+            if m in EARLY:
+                regroup_weights(EARLY[m], 1)
+                quantise_weights(EARLY[m], 0)
+            if m - 1 in EARLY:
+                quantise_weights(EARLY[m - 1], 1)
         quantise_own(TILES - 1)
 
-        load_weight_chunk(W_ROW_BUFFERS)
-        for g in range(PASSES):
-            if g > 0:
-                regroup_weight_chunk(g)
-                quantise_weight_chunk(g)
+        pieces = [(c, half) for c in range(CHUNKS) for half in range(HALVES)]
+        done = HALVES * len(EARLY)
+        regroup_weights(*pieces[done])
+
+        def next_piece(i):
+            if i + 1 < len(pieces):
+                regroup_weights(*pieces[i + 1])
+            quantise_weights(*pieces[i])
+
+        for i in range(HALVES * PASSES):
+            if i >= done:
+                next_piece(i)
             for m in range(FIRST):
-                multiply(m, OWN, g)
-        regroup_weight_chunk(PASSES)
+                multiply(m, OWN, *pieces[i])
         for m in range(FIRST):
             set_aside(m)
-        for g in range(PASSES):
-            quantise_weight_chunk(PASSES * AGG + g)
+        i = HALVES * PASSES
+        next_piece(i)
         for m in range(FIRST, TILES):
             for g in range(PASSES):
-                multiply(m, OWN, g)
+                for half in range(HALVES):
+                    multiply(m, OWN, g, half)
+            for j in range(HALVES):
+                i += 1
+                if i < len(pieces):
+                    next_piece(i)
             set_aside(m)
 
-        for m in range(ROW_BUFFERS):
-            load_neigh_rows(m)
         for m in range(TILES + 1):
             if m < TILES:
                 for g in range(PASSES):
                     prepare_agg(m, g)
-                if m + ROW_BUFFERS < TILES:
-                    load_neigh_rows(m + ROW_BUFFERS)
-            if m > 0:
+            if m == TILES:
+                for half in range(HALVES):
+                    for g in range(PASSES):
+                        multiply(m - 1, AGG, g, half)
+                    finish(m - 1, half)
+                    rectify(m - 1, slice(half * N_TILE, (half + 1) * N_TILE))
+            elif m > 0:
                 for g in range(PASSES):
-                    multiply(m - 1, AGG, g)
-                finish(m - 1)
+                    for half in range(HALVES):
+                        multiply(m - 1, AGG, g, half)
+                for half in range(HALVES):
+                    finish(m - 1, half)
+                rectify(m - 1, slice(0, H))
 
-        for m in range(TILES):
+        for m in range(TILES - 1):
             nc.sync.dma_start(out=out_view[m], in_=result[:, m, :])
+        for half in range(HALVES):
+            cols = slice(half * N_TILE, (half + 1) * N_TILE)
+            nc.sync.dma_start(out=out_view[TILES - 1][:, cols], in_=result[:, TILES - 1, cols])

@@ -177,13 +177,15 @@ def tile_graphsage_pa_kernel(tc, nf1, nf2, w1_0, w2_0, out):
                 in_=agg_grouped[:].rearrange("p r t -> p (r t)"),
             )
 
-        def multiply(m, product, g, half):
+        def half_cols(half):
+            return slice(half * N_TILE, (half + 1) * N_TILE)
+
+        def multiply(m, product, g, cols):
             if g == 0:
-                acc[m, product, half] = banks.tile([P, N_TILE], F32, name="acc", tag="bank")
+                acc[m, product, cols.start] = banks.tile([P, N_TILE], F32, name="acc", tag="bank")
             c = PASSES * product + g
-            cols = slice(half * N_TILE, (half + 1) * N_TILE)
             nc.tensor.matmul_mx(
-                out=acc[m, product, half][:],
+                out=acc[m, product, cols.start][:, : cols.stop - cols.start],
                 lhsT=x_codes[m, product][:, g, :].bitcast(FP8X4),
                 lhsT_scale=x_scales[m, product][:, g, :],
                 rhs=w_codes[:, c, cols].bitcast(FP8X4),
@@ -194,17 +196,25 @@ def tile_graphsage_pa_kernel(tc, nf1, nf2, w1_0, w2_0, out):
 
         def set_aside(m):
             nc.vector.tensor_copy(out=result[:, m, 0:N_TILE], in_=acc[m, OWN, 0][:])
-            nc.scalar.copy(out=result[:, m, N_TILE:H], in_=acc[m, OWN, 1][:])
+            nc.scalar.copy(out=result[:, m, N_TILE:H], in_=acc[m, OWN, N_TILE][:])
 
-        def finish(m, half):
-            cols = slice(half * N_TILE, (half + 1) * N_TILE)
+        def add_products(m, cols):
             nc.vector.tensor_add(
-                out=result[:, m, cols], in0=acc[m, AGG, half][:], in1=result[:, m, cols]
+                out=result[:, m, cols],
+                in0=acc[m, AGG, cols.start][:, : cols.stop - cols.start],
+                in1=result[:, m, cols],
             )
 
-        def rectify(m, cols):
+        def rectify_on_vector(m, cols):
             nc.vector.tensor_scalar_max(
                 out=result[:, m, cols], in0=result[:, m, cols], scalar1=0.0
+            )
+
+        def rectify_on_scalar(m, cols):
+            nc.scalar.activation(
+                out=result[:, m, cols],
+                in_=result[:, m, cols],
+                func=mybir.ActivationFunctionType.Relu,
             )
 
         for m in range(TILES):
@@ -242,7 +252,8 @@ def tile_graphsage_pa_kernel(tc, nf1, nf2, w1_0, w2_0, out):
             if i >= done:
                 next_piece(i)
             for m in range(FIRST):
-                multiply(m, OWN, *pieces[i])
+                c, half = pieces[i]
+                multiply(m, OWN, c, half_cols(half))
         for m in range(FIRST):
             set_aside(m)
         i = HALVES * PASSES
@@ -250,7 +261,7 @@ def tile_graphsage_pa_kernel(tc, nf1, nf2, w1_0, w2_0, out):
         for m in range(FIRST, TILES):
             for g in range(PASSES):
                 for half in range(HALVES):
-                    multiply(m, OWN, g, half)
+                    multiply(m, OWN, g, half_cols(half))
             for j in range(HALVES):
                 i += 1
                 if i < len(pieces):
@@ -261,22 +272,30 @@ def tile_graphsage_pa_kernel(tc, nf1, nf2, w1_0, w2_0, out):
             if m < TILES:
                 for g in range(PASSES):
                     prepare_agg(m, g)
-            if m == TILES:
-                for half in range(HALVES):
-                    for g in range(PASSES):
-                        multiply(m - 1, AGG, g, half)
-                    finish(m - 1, half)
-                    rectify(m - 1, slice(half * N_TILE, (half + 1) * N_TILE))
-            elif m > 0:
+            if 0 < m < TILES:
                 for g in range(PASSES):
                     for half in range(HALVES):
-                        multiply(m - 1, AGG, g, half)
+                        multiply(m - 1, AGG, g, half_cols(half))
                 for half in range(HALVES):
-                    finish(m - 1, half)
-                rectify(m - 1, slice(0, H))
+                    add_products(m - 1, half_cols(half))
+                    if m == TILES - 1:
+                        rectify_on_scalar(m - 1, half_cols(half))
+                if m < TILES - 1:
+                    rectify_on_vector(m - 1, slice(0, H))
+        last = TILES - 1
+        last_pieces = [half_cols(0), slice(N_TILE, N_TILE + N_TILE // 2), slice(N_TILE + N_TILE // 2, H)]
+        for cols in last_pieces:
+            for g in range(PASSES):
+                multiply(last, AGG, g, cols)
+            add_products(last, cols)
+            if cols.stop < H:
+                rectify_on_scalar(last, cols)
+            else:
+                rectify_on_vector(last, cols)
 
-        for m in range(TILES - 1):
+        for m in range(TILES - 2):
             nc.sync.dma_start(out=out_view[m], in_=result[:, m, :])
-        for half in range(HALVES):
-            cols = slice(half * N_TILE, (half + 1) * N_TILE)
-            nc.sync.dma_start(out=out_view[TILES - 1][:, cols], in_=result[:, TILES - 1, cols])
+        for cols in [half_cols(0), half_cols(1)]:
+            nc.sync.dma_start(out=out_view[TILES - 2][:, cols], in_=result[:, TILES - 2, cols])
+        for cols in last_pieces:
+            nc.sync.dma_start(out=out_view[last][:, cols], in_=result[:, last, cols])

@@ -32,6 +32,8 @@ PASSES_PER_BANK = 2
 ROW_BUFFERS = 4
 W_ROW_BUFFERS = 4
 FIRST = PSUM_BANKS // HALVES
+SHARED = (4, 5, 6, 7)
+VECTOR_PASS = PASSES - 1
 EARLY = {1: 0, 3: 1}
 
 FLOPS = 2 * 2 * NODES * D * H
@@ -42,6 +44,7 @@ def tile_graphsage_pa_kernel(tc, nf1, nf2, w1_0, w2_0, out):
 
     own_view = nf1.rearrange("(m p) d -> m p d", p=P)
     neigh_view = nf2.rearrange("(m q p) d -> m p q d", q=NEIGHBOURS, p=P)
+    neigh_by_node_view = nf2.rearrange("(m p q) d -> m p q d", q=NEIGHBOURS, p=P)
     out_view = out.rearrange("(m p) h -> m p h", p=P)
     own_w_view = w2_0.rearrange("(g p t) n -> g p t n", t=PACK, p=P)
     agg_w_view = w1_0.rearrange("(g p t) n -> g p t n", t=PACK, p=P)
@@ -77,6 +80,7 @@ def tile_graphsage_pa_kernel(tc, nf1, nf2, w1_0, w2_0, out):
         result = keep.tile([P, TILES, H], F32)
 
         own_rows, neigh_rows, w_rows, w_grouped, own_grouped = {}, {}, {}, {}, {}
+        agg_rows = {}
         x_codes, x_scales, acc = {}, {}, {}
 
         def load_own_rows(m):
@@ -89,10 +93,18 @@ def tile_graphsage_pa_kernel(tc, nf1, nf2, w1_0, w2_0, out):
         def load_neigh_rows(m):
             row_buffer = rows_pool.tile([P, NEIGHBOURS, D], BF16)
             neigh_rows[m] = row_buffer
-            nc.sync.dma_start(out=row_buffer[:], in_=neigh_view[m])
+            if m in SHARED:
+                rest = slice(VECTOR_PASS * K_PASS, D)
+                nc.sync.dma_start(
+                    out=row_buffer[:, :, rest], in_=neigh_by_node_view[m][:, :, rest]
+                )
+                first = slice(0, VECTOR_PASS * K_PASS)
+                nc.sync.dma_start(out=row_buffer[:, :, first], in_=neigh_view[m][:, :, first])
+            else:
+                nc.sync.dma_start(out=row_buffer[:], in_=neigh_view[m])
 
         def load_weight_chunk(c):
-            rows = w_rows_pool.tile([P, PACK, H], BF16)
+            rows = w_rows_pool.tile([P, PACK, H], BF16, tag="w_rows")
             for half in range(HALVES):
                 w_rows[c, half] = rows[:, :, half * N_TILE : (half + 1) * N_TILE]
             nc.sync.dma_start(
@@ -151,12 +163,65 @@ def tile_graphsage_pa_kernel(tc, nf1, nf2, w1_0, w2_0, out):
                 in_=own_grouped[m][:],
             )
 
+        def mean_on_vector(m, g):
+            features = slice(g * K_PASS, (g + 1) * K_PASS)
+            rows = neigh_rows[m][:, :, features]
+            total = w_rows_pool.tile([P, K_PASS], F32, tag="w_rows")
+            agg_rows[m] = agg_grouped_pool.tile(
+                [P, 2, P, 2], BF16, name="agg_grouped", align_bytes=64
+            )
+            nc.scalar.activation(
+                out=total[:],
+                in_=rows[:, 0],
+                func=mybir.ActivationFunctionType.Copy,
+                scale=1.0 / NEIGHBOURS,
+            )
+            for q in range(1, NEIGHBOURS - 1):
+                nc.vector.scalar_tensor_tensor(
+                    out=total[:],
+                    in0=rows[:, q],
+                    scalar=1.0 / NEIGHBOURS,
+                    in1=total[:],
+                    op0=mybir.AluOpType.mult,
+                    op1=mybir.AluOpType.add,
+                )
+            last_rows = rows[:, NEIGHBOURS - 1].rearrange("n (p u e) -> n u p e", u=2, e=2)
+            parts = total[:].rearrange("n (p u e) -> n u p e", u=2, e=2)
+            for u in range(2):
+                nc.vector.scalar_tensor_tensor(
+                    out=agg_rows[m][:, u],
+                    in0=last_rows[:, u],
+                    scalar=1.0 / NEIGHBOURS,
+                    in1=parts[:, u],
+                    op0=mybir.AluOpType.mult,
+                    op1=mybir.AluOpType.add,
+                )
+
+        def transpose_agg(m, g):
+            words = agg_rows[m][:].rearrange("n u p e -> n (u p e)").bitcast(F32)
+            agg_bank = banks.tile([P, 2, P], F32, tag="bank")
+            for u in range(2):
+                nc.tensor.transpose(agg_bank[:, u, :], words[:, u * P : (u + 1) * P], ident[:])
+            agg_grouped = agg_grouped_pool.tile([P, P * PACK], BF16, align_bytes=64)
+            nc.scalar.copy(
+                out=agg_grouped[:].bitcast(F32).rearrange("p (r u) -> p r u", u=2),
+                in_=agg_bank[:].rearrange("p u r -> p r u"),
+            )
+            nc.vector.quantize_mx(
+                out=x_codes[m, AGG][:, g, :].bitcast(FP8X4),
+                scales=x_scales[m, AGG][:, g, :],
+                in_=agg_grouped[:],
+            )
+
         def prepare_agg(m, g):
             if g == 0:
                 agg_codes = agg_mx_pool.tile([P, PASSES, P], U32, align_bytes=64)
                 agg_scales = agg_mx_pool.tile([P, PASSES, P], U8, align_bytes=64)
                 x_codes[m, AGG] = agg_codes[:]
                 x_scales[m, AGG] = agg_scales[:]
+            if m in SHARED and g == VECTOR_PASS:
+                transpose_agg(m, g)
+                return
             agg_bank = banks.tile([P, PACK, P], F32, tag="bank")
             for q in range(NEIGHBOURS):
                 nodes = slice(q * NODES_PER_ROWS, (q + 1) * NODES_PER_ROWS)
@@ -272,6 +337,8 @@ def tile_graphsage_pa_kernel(tc, nf1, nf2, w1_0, w2_0, out):
             if m < TILES:
                 for g in range(PASSES):
                     prepare_agg(m, g)
+                if m + 1 in SHARED:
+                    mean_on_vector(m + 1, VECTOR_PASS)
             if 0 < m < TILES:
                 for g in range(PASSES):
                     for half in range(HALVES):

@@ -32,6 +32,7 @@ PASSES_PER_BANK = 2
 ROW_BUFFERS = 4
 W_ROW_BUFFERS = 4
 FIRST = PSUM_BANKS // HALVES
+LAST_CHUNK = CHUNKS - 1
 SHARED = (4, 5, 6, 7)
 VECTOR_PASS = PASSES - 1
 EARLY = {1: 0, 3: 1}
@@ -56,7 +57,7 @@ def tile_graphsage_pa_kernel(tc, nf1, nf2, w1_0, w2_0, out):
         w_rows_pool = ctx.enter_context(tc.tile_pool(name="w_rows", bufs=W_ROW_BUFFERS))
         w_grouped_pool = ctx.enter_context(tc.tile_pool(name="w_grouped", bufs=6))
         own_grouped_pool = ctx.enter_context(tc.tile_pool(name="own_grouped", bufs=3))
-        agg_grouped_pool = ctx.enter_context(tc.tile_pool(name="agg_grouped", bufs=4))
+        agg_grouped_pool = ctx.enter_context(tc.tile_pool(name="agg_grouped", bufs=7))
         agg_mx_pool = ctx.enter_context(tc.tile_pool(name="agg_mx", bufs=2))
         banks = ctx.enter_context(tc.psum_pool(name="banks", bufs=PSUM_BANKS))
         ctx.enter_context(tc.manual_schedule())
@@ -286,9 +287,12 @@ def tile_graphsage_pa_kernel(tc, nf1, nf2, w1_0, w2_0, out):
             if m in EARLY:
                 load_weight_chunk(EARLY[m])
             load_own_rows(m)
-        for c in range(len(EARLY), CHUNKS):
+        for c in range(len(EARLY), LAST_CHUNK):
             load_weight_chunk(c)
-        for m in range(TILES):
+        load_neigh_rows(0)
+        load_neigh_rows(1)
+        load_weight_chunk(LAST_CHUNK)
+        for m in range(2, TILES):
             load_neigh_rows(m)
 
         for m in range(TILES):
@@ -304,7 +308,7 @@ def tile_graphsage_pa_kernel(tc, nf1, nf2, w1_0, w2_0, out):
                 quantise_weights(EARLY[m - 1], 1)
         quantise_own(TILES - 1)
 
-        pieces = [(c, half) for c in range(CHUNKS) for half in range(HALVES)]
+        pieces = [(c, half) for c in range(LAST_CHUNK) for half in range(HALVES)]
         done = HALVES * len(EARLY)
         regroup_weights(*pieces[done])
 
@@ -337,6 +341,11 @@ def tile_graphsage_pa_kernel(tc, nf1, nf2, w1_0, w2_0, out):
             if m < TILES:
                 for g in range(PASSES):
                     prepare_agg(m, g)
+                if m == 0:
+                    for half in range(HALVES):
+                        regroup_weights(LAST_CHUNK, half)
+                    for half in range(HALVES):
+                        quantise_weights(LAST_CHUNK, half)
                 if m + 1 in SHARED:
                     mean_on_vector(m + 1, VECTOR_PASS)
             if 0 < m < TILES:

@@ -340,14 +340,14 @@ def tile_graphsage_pa_kernel(tc, nf1, nf2, w1_0, w2_0, out):
         for m in range(TILES + 1):
             if m < TILES:
                 for g in range(PASSES):
+                    if g == PASSES // 2 and m + 1 in SHARED:
+                        mean_on_vector(m + 1, VECTOR_PASS)
                     prepare_agg(m, g)
                 if m == 0:
                     for half in range(HALVES):
                         regroup_weights(LAST_CHUNK, half)
                     for half in range(HALVES):
                         quantise_weights(LAST_CHUNK, half)
-                if m + 1 in SHARED:
-                    mean_on_vector(m + 1, VECTOR_PASS)
             if 0 < m < TILES:
                 for g in range(PASSES):
                     for half in range(HALVES):

from contextlib import ExitStack

import concourse.mybir as mybir
from concourse.masks import make_identity

F32 = mybir.dt.float32
BF16 = mybir.dt.bfloat16
U32 = mybir.dt.uint32
U8 = mybir.dt.uint8
FP8X4 = mybir.dt.float8_e4m3fn_x4

P = 128
PACK = 4
K_PASS = P * PACK
PSUM_BANKS = 8
N_TILE = 512

NODES = 1024
NEIGHBOURS = 4
D = 2048
H = 1024

TILES = NODES // P
PASSES = D // K_PASS
OWN, AGG = 0, 1
CHUNKS = 2 * PASSES
HALVES = H // N_TILE
NODES_PER_ROWS = P // NEIGHBOURS
WORDS_PER_PASS = K_PASS // 2
PASSES_PER_BANK = 2

ROW_BUFFERS = 4
W_ROW_BUFFERS = 4
FIRST = PSUM_BANKS // HALVES
LAST_CHUNK = CHUNKS - 1
SHARED = (4, 5, 6, 7)
VECTOR_PASS = PASSES - 1
EARLY = {1: 0, 3: 1}

FLOPS = 2 * 2 * NODES * D * H


def tile_graphsage_pa_kernel(tc, nf1, nf2, w1_0, w2_0, out):
    nc = tc.nc

    own_view = nf1.rearrange("(m p) d -> m p d", p=P)
    neigh_view = nf2.rearrange("(m q p) d -> m p q d", q=NEIGHBOURS, p=P)
    neigh_by_node_view = nf2.rearrange("(m p q) d -> m p q d", q=NEIGHBOURS, p=P)
    out_view = out.rearrange("(m p) h -> m p h", p=P)
    own_w_view = w2_0.rearrange("(g p t) n -> g p t n", t=PACK, p=P)
    agg_w_view = w1_0.rearrange("(g p t) n -> g p t n", t=PACK, p=P)

    with ExitStack() as ctx:
        const = ctx.enter_context(tc.tile_pool(name="const", bufs=1))
        keep = ctx.enter_context(tc.tile_pool(name="keep", bufs=1))
        rows_pool = ctx.enter_context(tc.tile_pool(name="rows", bufs=ROW_BUFFERS))
        w_rows_pool = ctx.enter_context(tc.tile_pool(name="w_rows", bufs=W_ROW_BUFFERS))
        w_grouped_pool = ctx.enter_context(tc.tile_pool(name="w_grouped", bufs=6))
        own_grouped_pool = ctx.enter_context(tc.tile_pool(name="own_grouped", bufs=3))
        agg_grouped_pool = ctx.enter_context(tc.tile_pool(name="agg_grouped", bufs=7))
        agg_mx_pool = ctx.enter_context(tc.tile_pool(name="agg_mx", bufs=2))
        banks = ctx.enter_context(tc.psum_pool(name="banks", bufs=PSUM_BANKS))
        ctx.enter_context(tc.manual_schedule())

        ident = const.tile([P, P], F32)
        make_identity(nc, ident[:])
        mean_f32 = const.tile([P, NODES_PER_ROWS], F32)
        nc.vector.tensor_reduce(
            out=mean_f32[:],
            in_=ident[:].rearrange("p (i j) -> p i j", j=NEIGHBOURS),
            axis=mybir.AxisListType.X,
            op=mybir.AluOpType.add,
        )
        mean_cols = const.tile([P, NODES_PER_ROWS], BF16)
        nc.vector.tensor_scalar_mul(out=mean_cols[:], in0=mean_f32[:], scalar1=1.0 / NEIGHBOURS)

        w_codes = keep.tile([P, CHUNKS, H], U32, align_bytes=64)
        w_scales = keep.tile([P, CHUNKS, H], U8, align_bytes=64)
        own_codes = keep.tile([P, TILES, PASSES, P], U32, align_bytes=64)
        own_scales = keep.tile([P, TILES, PASSES, P], U8, align_bytes=64)
        result = keep.tile([P, TILES, H], F32)

        own_rows, neigh_rows, w_rows, w_grouped, own_grouped = {}, {}, {}, {}, {}
        agg_rows = {}
        x_codes, x_scales, acc = {}, {}, {}

        def load_own_rows(m):
            if m % NEIGHBOURS == 0:
                row_buffer = rows_pool.tile([P, NEIGHBOURS, D], BF16)
                for j in range(NEIGHBOURS):
                    own_rows[m + j] = row_buffer[:, j, :]
            nc.sync.dma_start(out=own_rows[m], in_=own_view[m])

        def load_neigh_rows(m):
            row_buffer = rows_pool.tile([P, NEIGHBOURS, D], BF16)
            neigh_rows[m] = row_buffer
            if m in SHARED:
                rest = slice(VECTOR_PASS * K_PASS, D)
                nc.sync.dma_start(
                    out=row_buffer[:, :, rest], in_=neigh_by_node_view[m][:, :, rest]
                )
                first = slice(0, VECTOR_PASS * K_PASS)
                nc.sync.dma_start(out=row_buffer[:, :, first], in_=neigh_view[m][:, :, first])
            else:
                nc.sync.dma_start(out=row_buffer[:], in_=neigh_view[m])

        def load_weight_chunk(c):
            rows = w_rows_pool.tile([P, PACK, H], BF16, tag="w_rows")
            for half in range(HALVES):
                w_rows[c, half] = rows[:, :, half * N_TILE : (half + 1) * N_TILE]
            nc.sync.dma_start(
                out=rows[:], in_=own_w_view[c] if c < PASSES else agg_w_view[c - PASSES]
            )

        def regroup_weights(c, half):
            w_grouped[c, half] = w_grouped_pool.tile(
                [P, N_TILE, PACK], BF16, name="w_grouped", align_bytes=64
            )
            grouped = w_grouped[c, half][:].rearrange("p (a i) t -> p a t i", i=4)
            rows = w_rows[c, half].rearrange("p t (a i) -> p a t i", i=4)
            middle = N_TILE // 4 // 2
            nc.vector.tensor_copy(out=grouped[:, :middle], in_=rows[:, :middle])
            nc.scalar.copy(out=grouped[:, middle:], in_=rows[:, middle:])

        def quantise_weights(c, half):
            cols = slice(half * N_TILE, (half + 1) * N_TILE)
            nc.vector.quantize_mx(
                out=w_codes[:, c, cols].bitcast(FP8X4),
                scales=w_scales[:, c, cols],
                in_=w_grouped[c, half][:].rearrange("p n t -> p (n t)"),
            )

        def transpose_own(m):
            row_words = own_rows[m].bitcast(F32)
            own_grouped[m] = own_grouped_pool.tile(
                [P, PASSES * P * PACK], BF16, name="own_grouped", align_bytes=64
            )
            grouped_words = own_grouped[m][:].bitcast(F32).rearrange(
                "p (g r u) -> p g r u", g=PASSES, u=2
            )
            for first_pass in range(0, PASSES, PASSES_PER_BANK):
                own_bank = banks.tile([P, PASSES_PER_BANK, 2, P], F32, tag="bank")
                for i in range(PASSES_PER_BANK):
                    for u in range(2):
                        first_word = (first_pass + i) * WORDS_PER_PASS
                        nc.tensor.transpose(
                            own_bank[:, i, u, :],
                            row_words[:, first_word + u : first_word + WORDS_PER_PASS : 2],
                            ident[:],
                        )
                on_vector = m % 2 == 0 and first_pass > 0
                copy = nc.vector.tensor_copy if on_vector else nc.scalar.copy
                copy(
                    out=grouped_words[:, first_pass : first_pass + PASSES_PER_BANK],
                    in_=own_bank[:].rearrange("p g u r -> p g r u"),
                )

        def quantise_own(m):
            x_codes[m, OWN] = own_codes[:, m]
            x_scales[m, OWN] = own_scales[:, m]
            nc.vector.quantize_mx(
                out=x_codes[m, OWN].rearrange("p g r -> p (g r)").bitcast(FP8X4),
                scales=x_scales[m, OWN].rearrange("p g r -> p (g r)"),
                in_=own_grouped[m][:],
            )

        def mean_on_vector(m, g):
            features = slice(g * K_PASS, (g + 1) * K_PASS)
            rows = neigh_rows[m][:, :, features]
            total = w_rows_pool.tile([P, K_PASS], F32, tag="w_rows")
            agg_rows[m] = agg_grouped_pool.tile(
                [P, 2, P, 2], BF16, name="agg_grouped", align_bytes=64
            )
            nc.scalar.activation(
                out=total[:],
                in_=rows[:, 0],
                func=mybir.ActivationFunctionType.Copy,
                scale=1.0 / NEIGHBOURS,
            )
            for q in range(1, NEIGHBOURS - 1):
                nc.vector.scalar_tensor_tensor(
                    out=total[:],
                    in0=rows[:, q],
                    scalar=1.0 / NEIGHBOURS,
                    in1=total[:],
                    op0=mybir.AluOpType.mult,
                    op1=mybir.AluOpType.add,
                )
            last_rows = rows[:, NEIGHBOURS - 1].rearrange("n (p u e) -> n u p e", u=2, e=2)
            parts = total[:].rearrange("n (p u e) -> n u p e", u=2, e=2)
            for u in range(2):
                nc.vector.scalar_tensor_tensor(
                    out=agg_rows[m][:, u],
                    in0=last_rows[:, u],
                    scalar=1.0 / NEIGHBOURS,
                    in1=parts[:, u],
                    op0=mybir.AluOpType.mult,
                    op1=mybir.AluOpType.add,
                )

        def transpose_agg(m, g):
            words = agg_rows[m][:].rearrange("n u p e -> n (u p e)").bitcast(F32)
            agg_bank = banks.tile([P, 2, P], F32, tag="bank")
            for u in range(2):
                nc.tensor.transpose(agg_bank[:, u, :], words[:, u * P : (u + 1) * P], ident[:])
            agg_grouped = agg_grouped_pool.tile([P, P * PACK], BF16, align_bytes=64)
            nc.scalar.copy(
                out=agg_grouped[:].bitcast(F32).rearrange("p (r u) -> p r u", u=2),
                in_=agg_bank[:].rearrange("p u r -> p r u"),
            )
            nc.vector.quantize_mx(
                out=x_codes[m, AGG][:, g, :].bitcast(FP8X4),
                scales=x_scales[m, AGG][:, g, :],
                in_=agg_grouped[:],
            )

        def prepare_agg(m, g):
            if g == 0:
                agg_codes = agg_mx_pool.tile([P, PASSES, P], U32, align_bytes=64)
                agg_scales = agg_mx_pool.tile([P, PASSES, P], U8, align_bytes=64)
                x_codes[m, AGG] = agg_codes[:]
                x_scales[m, AGG] = agg_scales[:]
            if m in SHARED and g == VECTOR_PASS:
                transpose_agg(m, g)
                return
            agg_bank = banks.tile([P, PACK, P], F32, tag="bank")
            for q in range(NEIGHBOURS):
                nodes = slice(q * NODES_PER_ROWS, (q + 1) * NODES_PER_ROWS)
                for t in range(PACK):
                    first_d = g * K_PASS
                    nc.tensor.matmul(
                        out=agg_bank[:, t, nodes],
                        lhsT=neigh_rows[m][:, q, first_d + t : first_d + K_PASS : PACK],
                        rhs=mean_cols[:],
                        start=True,
                        stop=True,
                    )
            agg_grouped = agg_grouped_pool.tile([P, P, PACK], BF16, align_bytes=64)
            nc.scalar.copy(out=agg_grouped[:], in_=agg_bank[:].rearrange("p t r -> p r t"))
            nc.vector.quantize_mx(
                out=x_codes[m, AGG][:, g, :].bitcast(FP8X4),
                scales=x_scales[m, AGG][:, g, :],
                in_=agg_grouped[:].rearrange("p r t -> p (r t)"),
            )

        def half_cols(half):
            return slice(half * N_TILE, (half + 1) * N_TILE)

        def multiply(m, product, g, cols):
            if g == 0:
                acc[m, product, cols.start] = banks.tile([P, N_TILE], F32, name="acc", tag="bank")
            c = PASSES * product + g
            nc.tensor.matmul_mx(
                out=acc[m, product, cols.start][:, : cols.stop - cols.start],
                lhsT=x_codes[m, product][:, g, :].bitcast(FP8X4),
                lhsT_scale=x_scales[m, product][:, g, :],
                rhs=w_codes[:, c, cols].bitcast(FP8X4),
                rhs_scale=w_scales[:, c, cols],
                start=(g == 0),
                stop=(g == PASSES - 1),
            )

        def set_aside(m):
            nc.vector.tensor_copy(out=result[:, m, 0:N_TILE], in_=acc[m, OWN, 0][:])
            nc.scalar.copy(out=result[:, m, N_TILE:H], in_=acc[m, OWN, N_TILE][:])

        def add_products(m, cols):
            nc.vector.tensor_add(
                out=result[:, m, cols],
                in0=acc[m, AGG, cols.start][:, : cols.stop - cols.start],
                in1=result[:, m, cols],
            )

        def rectify_on_vector(m, cols):
            nc.vector.tensor_scalar_max(
                out=result[:, m, cols], in0=result[:, m, cols], scalar1=0.0
            )

        def rectify_on_scalar(m, cols):
            nc.scalar.activation(
                out=result[:, m, cols],
                in_=result[:, m, cols],
                func=mybir.ActivationFunctionType.Relu,
            )

        for m in range(TILES):
            if m in EARLY:
                load_weight_chunk(EARLY[m])
            load_own_rows(m)
        for c in range(len(EARLY), LAST_CHUNK):
            load_weight_chunk(c)
        load_neigh_rows(0)
        load_neigh_rows(1)
        load_weight_chunk(LAST_CHUNK)
        for m in range(2, TILES):
            load_neigh_rows(m)

        for m in range(TILES):
            transpose_own(m)
            if m > 0:
                quantise_own(m - 1)
            if m + 1 in EARLY:
                regroup_weights(EARLY[m + 1], 0)
            if m in EARLY:
                regroup_weights(EARLY[m], 1)
                quantise_weights(EARLY[m], 0)
            if m - 1 in EARLY:
                quantise_weights(EARLY[m - 1], 1)
        quantise_own(TILES - 1)

        pieces = [(c, half) for c in range(LAST_CHUNK) for half in range(HALVES)]
        done = HALVES * len(EARLY)
        regroup_weights(*pieces[done])

        def next_piece(i):
            if i + 1 < len(pieces):
                regroup_weights(*pieces[i + 1])
            quantise_weights(*pieces[i])

        for i in range(HALVES * PASSES):
            if i >= done:
                next_piece(i)
            for m in range(FIRST):
                c, half = pieces[i]
                multiply(m, OWN, c, half_cols(half))
        for m in range(FIRST):
            set_aside(m)
        i = HALVES * PASSES
        next_piece(i)
        for m in range(FIRST, TILES):
            for g in range(PASSES):
                for half in range(HALVES):
                    multiply(m, OWN, g, half_cols(half))
            for j in range(HALVES):
                i += 1
                if i < len(pieces):
                    next_piece(i)
            set_aside(m)

        for m in range(TILES + 1):
            if m < TILES:
                for g in range(PASSES):
                    if g == PASSES // 2 and m + 1 in SHARED:
                        mean_on_vector(m + 1, VECTOR_PASS)
                    prepare_agg(m, g)
                if m == 0:
                    for half in range(HALVES):
                        regroup_weights(LAST_CHUNK, half)
                    for half in range(HALVES):
                        quantise_weights(LAST_CHUNK, half)
            if 0 < m < TILES:
                for g in range(PASSES):
                    for half in range(HALVES):
                        multiply(m - 1, AGG, g, half_cols(half))
                for half in range(HALVES):
                    add_products(m - 1, half_cols(half))
                    if m == TILES - 1:
                        rectify_on_scalar(m - 1, half_cols(half))
                if m < TILES - 1:
                    rectify_on_vector(m - 1, slice(0, H))
        last = TILES - 1
        last_pieces = [half_cols(0), slice(N_TILE, N_TILE + N_TILE // 2), slice(N_TILE + N_TILE // 2, H)]
        for cols in last_pieces:
            for g in range(PASSES):
                multiply(last, AGG, g, cols)
            add_products(last, cols)
            if cols.stop < H:
                rectify_on_scalar(last, cols)
            else:
                rectify_on_vector(last, cols)

        for m in range(TILES - 2):
            nc.sync.dma_start(out=out_view[m], in_=result[:, m, :])
        for cols in [half_cols(0), half_cols(1)]:
            nc.sync.dma_start(out=out_view[TILES - 2][:, cols], in_=result[:, TILES - 2, cols])
        for cols in last_pieces:
            nc.sync.dma_start(out=out_view[last][:, cols], in_=result[:, last, cols])
